import numpy as np
import ml_dtypes


def mxq(x, axis, fmt="e4m3"):
    dtype, down = {"e4m3": (ml_dtypes.float8_e4m3fn, 7), "e5m2": (ml_dtypes.float8_e5m2, 14)}[fmt]
    v = np.moveaxis(np.asarray(x, np.float32).astype(ml_dtypes.bfloat16).astype(np.float64), axis, -1)
    blocks = v.reshape(v.shape[:-1] + (-1, 32))
    amax = np.abs(blocks).max(-1, keepdims=True)
    byte = np.maximum(np.where(amax > 0, np.frexp(amax)[1] - 1 + 127, 0) - down, 1)
    scale = np.exp2(byte - 127.0)
    codes = (blocks / scale).astype(np.float32).astype(dtype).astype(np.float64)
    return np.moveaxis((codes * scale).reshape(v.shape), -1, axis)


WIDE = False


def mx_kscale(k):
    if not WIDE:
        return np.ones(k)
    levels = np.array([10, -10, 5, -5, 0])
    if k % 512:
        return np.exp2(np.random.permutation(np.resize(levels, k // 32))).repeat(32)
    a = np.empty((k // 512, 16))
    for p in range(k // 512):
        a[p, :8] = np.random.permutation(np.resize(levels, 8))
        for g in range(8):
            far = levels[np.abs(levels - a[p, g]) >= 10]
            a[p, g + 8] = far[np.random.randint(len(far))]
    return np.exp2(a.ravel()).repeat(32)


BF16 = ml_dtypes.bfloat16


def bf(x):
    return np.asarray(x, np.float32).astype(BF16)


def f64(x):
    return np.asarray(x).astype(np.float64)


N, H, S, R, T = 12288, 1024, 4, 128, 256


def sigmoid(v):
    return 1.0 / (1.0 + np.exp(-v))


def setup_inputs():
    s, t = mx_kscale(H), mx_kscale(H)
    g = np.exp(np.random.standard_normal((S, N)))
    return {"encodings": bf(np.random.standard_normal((N, H)) * s),
            "alphas": bf(g / g.sum(axis=0, keepdims=True)),
            "W1": bf(np.random.standard_normal((S, H, H)) * 1.4 / np.sqrt(H) / s[None, :, None] * t[None, None, :]),
            "b1": bf(np.random.standard_normal((S, H)) * 0.3 * t[None, :]),
            "W2": bf(np.random.standard_normal((S, H, T)) * 2.0 / np.sqrt(H) / t[None, :, None]),
            "b2": bf(np.random.standard_normal((S, T)) * 0.5)}


def reference(encodings, alphas, W1, b1, W2, b2):
    h0 = np.maximum(f64(encodings), 0.0)
    h1 = np.maximum((mxq(h0, 1, "e4m3") @ mxq(f64(W1), 1, "e4m3")) + f64(b1)[:, None, :], 0.0)
    out = sigmoid((mxq(h1, 2, "e4m3") @ mxq(f64(W2), 1, "e4m3")) + f64(b2)[:, None, :])
    return np.sum(f64(alphas)[:, :, None] * out, axis=0)

@@ -1,0 +1,326 @@
+from contextlib import ExitStack
+
+import concourse.mybir as mybir
+from concourse.masks import make_identity
+
+N_TOK, HID, SRC, TGT = 12288, 1024, 4, 256
+FLOPS = 2 * N_TOK * HID * HID * SRC + 2 * N_TOK * HID * TGT * SRC
+
+F32 = mybir.dt.float32
+BF16 = mybir.dt.bfloat16
+U32 = mybir.dt.uint32
+U8 = mybir.dt.uint8
+FP8X4 = mybir.dt.float8_e4m3fn_x4
+ACT = mybir.ActivationFunctionType
+ALU = mybir.AluOpType
+
+P = 128
+BLK = 512
+NBLK = N_TOK // BLK
+STEPS = NBLK * SRC * 2
+S_IL = 48
+
+
+def tile_moe_pb_l_kernel(tc, encodings, alphas, W1, b1, W2, b2, out):
+    nc = tc.nc
+    with ExitStack() as ctx:
+        keep = ctx.enter_context(tc.tile_pool(name="keep", bufs=1))
+        stream = ctx.enter_context(tc.tile_pool(name="stream", bufs=2))
+        ps1_pool = ctx.enter_context(tc.psum_pool(name="ps1p", bufs=4))
+        ps2_pool = ctx.enter_context(tc.psum_pool(name="ps2p", bufs=2))
+        xt_pool = ctx.enter_context(tc.psum_pool(name="xtp", bufs=2))
+        ctx.enter_context(tc.manual_schedule())
+
+        w1c = keep.tile([P, SRC, 2, HID], U32, name="w1c", align_bytes=64)
+        w1s = keep.tile([P, SRC, 2, HID], U8, name="w1s", align_bytes=64)
+        w2c = keep.tile([P, SRC, 2 * TGT], U32, name="w2c", align_bytes=64)
+        w2s = keep.tile([P, SRC, 2 * TGT], U8, name="w2s", align_bytes=64)
+        ident = keep.tile([P, P], F32, name="ident")
+        ones = keep.tile([P, P], BF16, name="ones")
+        bz = keep.tile([P, SRC * TGT], BF16, name="bz")
+        b1raw = keep.tile([P, SRC, 16], BF16, name="b1raw")
+        b1col = keep.tile([P, SRC, 8], F32, name="b1col")
+        b2d = keep.tile([P, SRC, 2, TGT], F32, name="b2d")
+        a_sb = keep.tile([P, BLK], BF16, name="a_sb")
+        a32 = keep.tile([P, 4, P], F32, name="a32")
+        acol = keep.tile([P, 4, P], F32, name="acol")
+        warm = keep.tile([P, 1], F32, name="warm")
+
+        x_raw = {}
+        x_relu = {}
+        x_grp = {}
+        h0 = {}
+        w1raw = {}
+        w1grp = {}
+        w2raw = {}
+        w2grp = {}
+        h1r = {}
+        h1g = {}
+        h1q = {}
+        ps2 = {}
+        u_t = {}
+        acc = {}
+
+        def load_x(b):
+            t = stream.tile([P, 4 * HID], BF16, name="xraw", tag="xraw", bufs=2)
+            nc.sync.dma_start(out=t[:], in_=encodings[b * BLK:(b + 1) * BLK, :].rearrange("(p i) h -> p (i h)", i=4))
+            x_raw[b] = t
+
+        def relu_x(b):
+            t = x_raw.pop(b)
+            nc.vector.tensor_scalar_max(out=t[:], in0=t[:], scalar1=0.0)
+            x_relu[b] = t
+
+        def transpose_x(b, g, copy_engines):
+            words = x_relu[b][:].bitcast(F32)
+            if g == 0:
+                x_grp[b] = stream.tile([P, 2 * BLK * 4], BF16, name="xgrp", tag="xgrp", bufs=2, align_bytes=64)
+            gw = x_grp[b][:].bitcast(F32)
+            for ip in range(2):
+                xt = xt_pool.tile([P, 2, 2 * P], F32, name="xt", tag="xt")
+                for i2 in range(2):
+                    i = 2 * ip + i2
+                    for u in range(2):
+                        lo = 512 * i + 256 * g + u
+                        nc.tensor.transpose(xt[:, u, P * i2:P * (i2 + 1)], words[:, lo:lo + 255:2], ident[:])
+                dst = gw[:, 1024 * g + 512 * ip:1024 * g + 512 * (ip + 1)].rearrange("p (c u) -> p c u", u=2)
+                src = xt[:].rearrange("p u c -> p c u")
+                if copy_engines[ip] == "s":
+                    nc.scalar.copy(out=dst, in_=src)
+                else:
+                    nc.vector.tensor_copy(out=dst, in_=src)
+            if g == 1:
+                x_relu.pop(b)
+
+        def quant_x(b, g):
+            if g == 0:
+                hc = stream.tile([P, 2, BLK], U32, name="h0c", tag="h0c", bufs=2, align_bytes=64)
+                hs = stream.tile([P, 2, BLK], U8, name="h0s", tag="h0s", bufs=2, align_bytes=64)
+                h0[b] = (hc, hs)
+            hc, hs = h0[b]
+            nc.vector.quantize_mx(out=hc[:, g, :].bitcast(FP8X4), scales=hs[:, g, :],
+                                  in_=x_grp[b][:, 2048 * g:2048 * (g + 1)])
+            if g == 1:
+                x_grp.pop(b)
+
+        def load_w1(s, g):
+            t = stream.tile([P, 4 * HID], BF16, name="w1raw", tag="w1raw", bufs=4)
+            nc.sync.dma_start(out=t[:], in_=W1[s, 512 * g:512 * (g + 1), :].rearrange("(p j) c -> p (j c)", j=4))
+            w1raw[(s, g)] = t
+
+        def il_w1(eng, s, g, hh):
+            t = stream.tile([P, 2048], BF16, name="wgrp", tag="wgrp", bufs=4, align_bytes=64)
+            dst = t[:].rearrange("p (t m j) -> p t m j", t=4, j=4)
+            src = w1raw[(s, g)][:].rearrange("p (j c) -> p j c", j=4)[:, :, 512 * hh:512 * (hh + 1)].rearrange(
+                "p j (m t) -> p t m j", t=4)
+            if eng == "v":
+                nc.vector.tensor_copy(out=dst, in_=src)
+            elif eng == "s":
+                nc.scalar.copy(out=dst, in_=src)
+            else:
+                nc.gpsimd.tensor_scalar(out=dst, in0=src, scalar1=1.0, scalar2=0.0, op0=ALU.mult, op1=ALU.add)
+            w1grp[(s, g, hh)] = t
+
+        def q_w1(s, g, hh):
+            cols = (512 * hh, 512 * (hh + 1))
+            nc.vector.quantize_mx(out=w1c[:, s, g, cols[0]:cols[1]].bitcast(FP8X4),
+                                  scales=w1s[:, s, g, cols[0]:cols[1]], in_=w1grp.pop((s, g, hh))[:])
+
+        def load_w2(s):
+            t = stream.tile([P, 2, 4 * TGT], BF16, name="w2raw", tag="w2raw", bufs=2)
+            nc.sync.dma_start(out=t[:], in_=W2[s, :, :].rearrange("(g p j) t -> p g (j t)", g=2, j=4))
+            w2raw[s] = t
+
+        def il_w2(eng, s):
+            t = stream.tile([P, 2048], BF16, name="w2grp", tag="w2grp", bufs=2, align_bytes=64)
+            dst = t[:].rearrange("p (g t j) -> p g t j", g=2, j=4)
+            src = w2raw.pop(s)[:].rearrange("p g (j t) -> p g t j", j=4)
+            if eng == "v":
+                nc.vector.tensor_copy(out=dst, in_=src)
+            else:
+                nc.gpsimd.tensor_scalar(out=dst, in0=src, scalar1=1.0, scalar2=0.0, op0=ALU.mult, op1=ALU.add)
+            w2grp[s] = t
+
+        def q_w2(s):
+            nc.vector.quantize_mx(out=w2c[:, s, :].bitcast(FP8X4), scales=w2s[:, s, :], in_=w2grp.pop(s)[:])
+
+        def stage1(hstep):
+            b, s, hh = hstep // 8, (hstep // 2) % 4, hstep % 2
+            hc, hs = h0[b]
+            r = stream.tile([P, 4, BLK], BF16, name="h1r", tag="h1r", bufs=3)
+            for t in range(4):
+                ps = ps1_pool.tile([P, BLK], F32, name="ps1", tag="ps1")
+                lo = 512 * hh + P * t
+                for g in range(2):
+                    nc.tensor.matmul_mx(out=ps[:], lhsT=w1c[:, s, g, lo:lo + P].bitcast(FP8X4),
+                                        lhsT_scale=w1s[:, s, g, lo:lo + P],
+                                        rhs=hc[:, g, :].bitcast(FP8X4), rhs_scale=hs[:, g, :],
+                                        start=(g == 0), stop=(g == 1))
+                nc.scalar.activation(out=r[:, t, :], in_=ps[:], func=ACT.Relu,
+                                     bias=b1col[:, s, 4 * hh + t:4 * hh + t + 1])
+            h1r[hstep] = r
+            if hstep % 8 == 7:
+                h0.pop(b)
+
+        def il_h1(hstep):
+            t = stream.tile([P, BLK, 4], BF16, name="h1g", tag="h1g", bufs=2, align_bytes=64)
+            src = h1r.pop(hstep)[:].rearrange("p t c -> p c t")
+            nc.vector.tensor_copy(out=t[:, 0:BLK - S_IL, :], in_=src[:, 0:BLK - S_IL, :])
+            if S_IL > 0:
+                nc.scalar.copy(out=t[:, BLK - S_IL:BLK, :], in_=src[:, BLK - S_IL:BLK, :])
+            h1g[hstep] = t
+
+        def q_h1(hstep):
+            c = stream.tile([P, BLK], U32, name="h1c", tag="h1c", bufs=6, align_bytes=64)
+            sc = stream.tile([P, BLK], U8, name="h1s", tag="h1s", bufs=6, align_bytes=64)
+            nc.vector.quantize_mx(out=c[:].bitcast(FP8X4), scales=sc[:],
+                                  in_=h1g.pop(hstep)[:].rearrange("p c t -> p (c t)"))
+            h1q[hstep] = (c, sc)
+
+        def stage2(q, ip):
+            s = q % 4
+            ps = ps2_pool.tile([P, 2, TGT], F32, name="ps2", tag="ps2")
+            for i2 in range(2):
+                lo = P * (2 * ip + i2)
+                for hh in range(2):
+                    c, sc = h1q[2 * q + hh]
+                    nc.tensor.matmul_mx(out=ps[:, i2, :], lhsT=c[:, lo:lo + P].bitcast(FP8X4),
+                                        lhsT_scale=sc[:, lo:lo + P],
+                                        rhs=w2c[:, s, TGT * hh:TGT * (hh + 1)].bitcast(FP8X4),
+                                        rhs_scale=w2s[:, s, TGT * hh:TGT * (hh + 1)],
+                                        start=(hh == 0), stop=(hh == 1))
+            ps2[(q, ip)] = ps
+            if ip == 1:
+                h1q.pop(2 * q)
+                h1q.pop(2 * q + 1)
+
+        def add_b2(q, ip):
+            t = stream.tile([P, 2, TGT], F32, name="u", tag="u", bufs=4)
+            nc.vector.tensor_tensor(out=t[:], in0=ps2.pop((q, ip))[:], in1=b2d[:, q % 4, :, :], op=ALU.add)
+            u_t[(q, ip)] = t
+
+        def sigmoid(q, ip):
+            t = u_t[(q, ip)]
+            nc.scalar.activation(out=t[:], in_=t[:], func=ACT.Sigmoid)
+
+        def wsum(q, ip):
+            b, s = q // 4, q % 4
+            if s == 0 and ip == 0:
+                acc[b] = stream.tile([P, 4, TGT], F32, name="acc", tag="acc", bufs=2)
+            a = acc[b]
+            t = u_t.pop((q, ip))
+            for i2 in range(2):
+                i = 2 * ip + i2
+                col = acol[:, i, NBLK * s + b:NBLK * s + b + 1]
+                if s == 0:
+                    nc.vector.tensor_scalar_mul(out=a[:, i, :], in0=t[:, i2, :], scalar1=col)
+                else:
+                    nc.vector.scalar_tensor_tensor(out=a[:, i, :], in0=t[:, i2, :], scalar=col, in1=a[:, i, :],
+                                                   op0=ALU.mult, op1=ALU.add)
+            if s == 3 and ip == 1:
+                nc.sync.dma_start(out=out[b * BLK:(b + 1) * BLK, :].rearrange("(p i) t -> p (i t)", i=4),
+                                  in_=acc.pop(b)[:].rearrange("p i t -> p (i t)"))
+
+        nc.vector.memset(warm[:], 0.0)
+        nc.vector.memset(bz[:], 0.0)
+        nc.vector.memset(a_sb[:], 0.0)
+        nc.vector.memset(ones[:], 1.0)
+        nc.scalar.dma_start(out=a_sb[0:96, :], in_=alphas.rearrange("s (b c) -> (s b) c", c=BLK))
+        nc.scalar.dma_start(out=bz[0:1, :], in_=b2.rearrange("(o s) t -> o (s t)", o=1))
+        for s in range(SRC):
+            nc.scalar.dma_start(out=b1raw[:, s, 0:8].rearrange("p (g t) -> p g t", g=2),
+                                in_=b1[s, :].rearrange("(g p t) -> p g t", g=2, t=4))
+        nc.scalar.activation(out=warm[:], in_=warm[:], func=ACT.Sigmoid)
+        load_x(0)
+        load_w1(0, 0)
+        load_w1(0, 1)
+        load_w1(1, 0)
+        load_w1(1, 1)
+        load_x(1)
+        load_w2(0)
+        make_identity(nc, ident[:])
+
+        nc.vector.tensor_copy(out=a32[:], in_=a_sb[:].rearrange("r (p i) -> r i p", i=4))
+        pa = xt_pool.tile([P, 4, P], F32, name="xt", tag="xt")
+        for i in range(4):
+            nc.tensor.transpose(pa[:, i, :], a32[:, i, :], ident[:])
+        nc.scalar.copy(out=acol[:], in_=pa[:])
+        for h in range(2):
+            pb = xt_pool.tile([P, 2, TGT], F32, name="xt", tag="xt")
+            nc.tensor.matmul(out=pb[:].rearrange("p s t -> p (s t)"), lhsT=ones[:], rhs=bz[:, 512 * h:512 * (h + 1)],
+                             start=True, stop=True)
+            for d in range(2):
+                nc.scalar.copy(out=b2d[:, 2 * h:2 * h + 2, d, :], in_=pb[:])
+        nc.vector.tensor_copy(out=b1col[:], in_=b1raw[:, :, 0:8])
+
+        relu_x(0)
+        transpose_x(0, 0, ("s", "s"))
+        il_w1("v", 0, 0, 0)
+        transpose_x(0, 1, ("s", "s"))
+        quant_x(0, 0)
+        q_w1(0, 0, 0)
+        il_w1("v", 0, 1, 0)
+        il_w1("s", 0, 0, 1)
+        quant_x(0, 1)
+        q_w1(0, 1, 0)
+        il_w1("s", 0, 1, 1)
+        q_w1(0, 0, 1)
+
+        for hs_i in range(STEPS + 6):
+            b, r8 = hs_i // 8, hs_i % 8
+            if hs_i == 0:
+                load_w2(1)
+                load_w1(2, 0)
+                load_w1(2, 1)
+            if hs_i == 2:
+                load_w2(2)
+                load_w1(3, 0)
+                load_w1(3, 1)
+            if hs_i == 4:
+                load_w2(3)
+            k = hs_i - 2
+            if k >= 3 and k < STEPS + 3:
+                sigmoid((k - 3) // 2, (k - 3) % 2)
+            k = hs_i - 1
+            if k >= 3 and k < STEPS + 3:
+                add_b2((k - 3) // 2, (k - 3) % 2)
+            if hs_i < STEPS:
+                stage1(hs_i)
+            if hs_i >= 1 and hs_i - 1 < STEPS:
+                il_h1(hs_i - 1)
+            k = hs_i - 3
+            if k >= 3 and k < STEPS + 3:
+                wsum((k - 3) // 2, (k - 3) % 2)
+            if hs_i >= 1 and hs_i - 1 < STEPS:
+                q_h1(hs_i - 1)
+            if hs_i >= 3 and hs_i < STEPS + 3:
+                stage2((hs_i - 3) // 2, (hs_i - 3) % 2)
+            if b + 1 < NBLK:
+                if r8 == 1:
+                    relu_x(b + 1)
+                if r8 == 2:
+                    transpose_x(b + 1, 0, ("s", "s"))
+                if r8 == 3:
+                    quant_x(b + 1, 0)
+                if r8 == 4:
+                    transpose_x(b + 1, 1, ("s", "s"))
+                if r8 == 5:
+                    quant_x(b + 1, 1)
+                    if b + 2 < NBLK:
+                        load_x(b + 2)
+            if hs_i == 0:
+                q_w1(0, 1, 1)
+                il_w2("v", 0)
+            if hs_i < 6:
+                s, hh = hs_i // 2 + 1, hs_i % 2
+                if hs_i >= 1:
+                    q_w1((hs_i - 1) // 2 + 1, 1, (hs_i - 1) % 2)
+                il_w1("v", s, 0, hh)
+                il_w1("s", s, 1, hh)
+                q_w1(s, 0, hh)
+            if hs_i == 6:
+                q_w1(3, 1, 1)
+            if hs_i < 8 and hs_i % 2 == 0 and hs_i >= 2:
+                il_w2("v", hs_i // 2)
+            if hs_i < 8 and hs_i % 2 == 1:
+                q_w2(hs_i // 2)

@@ -18,7 +18,7 @@ P = 128
 BLK = 512
 NBLK = N_TOK // BLK
 STEPS = NBLK * SRC * 2
-S_IL = 48
+S_IL = 0
 
 
 def tile_moe_pb_l_kernel(tc, encodings, alphas, W1, b1, W2, b2, out):
@@ -164,10 +164,12 @@ def tile_moe_pb_l_kernel(tc, encodings, alphas, W1, b1, W2, b2, out):
 
         def il_h1(hstep):
             t = stream.tile([P, BLK, 4], BF16, name="h1g", tag="h1g", bufs=2, align_bytes=64)
-            src = h1r.pop(hstep)[:].rearrange("p t c -> p c t")
-            nc.vector.tensor_copy(out=t[:, 0:BLK - S_IL, :], in_=src[:, 0:BLK - S_IL, :])
+            src = h1r.pop(hstep)[:].rearrange("p t (c i) -> p c t i", i=4)
+            dst = t[:].rearrange("p (c i) t -> p c t i", i=4)
+            cut = (BLK - S_IL) // 4
+            nc.vector.tensor_copy(out=dst[:, 0:cut, :, :], in_=src[:, 0:cut, :, :])
             if S_IL > 0:
-                nc.scalar.copy(out=t[:, BLK - S_IL:BLK, :], in_=src[:, BLK - S_IL:BLK, :])
+                nc.scalar.copy(out=dst[:, cut:BLK // 4, :, :], in_=src[:, cut:BLK // 4, :, :])
             h1g[hstep] = t
 
         def q_h1(hstep):
@@ -244,13 +246,13 @@ def tile_moe_pb_l_kernel(tc, encodings, alphas, W1, b1, W2, b2, out):
         pa = xt_pool.tile([P, 4, P], F32, name="xt", tag="xt")
         for i in range(4):
             nc.tensor.transpose(pa[:, i, :], a32[:, i, :], ident[:])
-        nc.scalar.copy(out=acol[:], in_=pa[:])
+        nc.vector.tensor_copy(out=acol[:], in_=pa[:])
         for h in range(2):
             pb = xt_pool.tile([P, 2, TGT], F32, name="xt", tag="xt")
             nc.tensor.matmul(out=pb[:].rearrange("p s t -> p (s t)"), lhsT=ones[:], rhs=bz[:, 512 * h:512 * (h + 1)],
                              start=True, stop=True)
             for d in range(2):
-                nc.scalar.copy(out=b2d[:, 2 * h:2 * h + 2, d, :], in_=pb[:])
+                nc.vector.tensor_copy(out=b2d[:, 2 * h:2 * h + 2, d, :], in_=pb[:])
         nc.vector.tensor_copy(out=b1col[:], in_=b1raw[:, :, 0:8])
 
         relu_x(0)

@@ -67,8 +67,9 @@ def tile_moe_pb_l_kernel(tc, encodings, alphas, W1, b1, W2, b2, out):
             x_raw[b] = t
 
         def relu_x(b):
-            t = x_raw.pop(b)
-            nc.vector.tensor_scalar_max(out=t[:], in0=t[:], scalar1=0.0)
+            t = stream.tile([P, 4 * HID], BF16, name="xsort", tag="xsort", bufs=2)
+            nc.vector.tensor_scalar_max(out=t[:].rearrange("p (u m e) -> p m u e", u=2, e=2),
+                                        in0=x_raw.pop(b)[:].rearrange("p (m u e) -> p m u e", u=2, e=2), scalar1=0.0)
             x_relu[b] = t
 
         def transpose_x(b, g, copy_engines):
@@ -81,8 +82,8 @@ def tile_moe_pb_l_kernel(tc, encodings, alphas, W1, b1, W2, b2, out):
                 for i2 in range(2):
                     i = 2 * ip + i2
                     for u in range(2):
-                        lo = 512 * i + 256 * g + u
-                        nc.tensor.transpose(xt[:, u, P * i2:P * (i2 + 1)], words[:, lo:lo + 255:2], ident[:])
+                        lo = 1024 * u + P * (2 * i + g)
+                        nc.tensor.transpose(xt[:, u, P * i2:P * (i2 + 1)], words[:, lo:lo + P], ident[:])
                 dst = gw[:, 1024 * g + 512 * ip:1024 * g + 512 * (ip + 1)].rearrange("p (c u) -> p c u", u=2)
                 src = xt[:].rearrange("p u c -> p c u")
                 if copy_engines[ip] == "s":
@@ -109,7 +110,7 @@ def tile_moe_pb_l_kernel(tc, encodings, alphas, W1, b1, W2, b2, out):
             w1raw[(s, g)] = t
 
         def il_w1(eng, s, g, hh):
-            t = stream.tile([P, 2048], BF16, name="wgrp", tag="wgrp", bufs=4, align_bytes=64)
+            t = stream.tile([P, 2048], BF16, name="wgrp", tag="wgrp", bufs=3, align_bytes=64)
             dst = t[:].rearrange("p (t m j) -> p t m j", t=4, j=4)
             src = w1raw[(s, g)][:].rearrange("p (j c) -> p j c", j=4)[:, :, 512 * hh:512 * (hh + 1)].rearrange(
                 "p j (m t) -> p t m j", t=4)
@@ -173,8 +174,8 @@ def tile_moe_pb_l_kernel(tc, encodings, alphas, W1, b1, W2, b2, out):
             h1g[hstep] = t
 
         def q_h1(hstep):
-            c = stream.tile([P, BLK], U32, name="h1c", tag="h1c", bufs=6, align_bytes=64)
-            sc = stream.tile([P, BLK], U8, name="h1s", tag="h1s", bufs=6, align_bytes=64)
+            c = stream.tile([P, BLK], U32, name="h1c", tag="h1c", bufs=5, align_bytes=64)
+            sc = stream.tile([P, BLK], U8, name="h1s", tag="h1s", bufs=5, align_bytes=64)
             nc.vector.quantize_mx(out=c[:].bitcast(FP8X4), scales=sc[:],
                                   in_=h1g.pop(hstep)[:].rearrange("p c t -> p (c t)"))
             h1q[hstep] = (c, sc)
@@ -197,7 +198,7 @@ def tile_moe_pb_l_kernel(tc, encodings, alphas, W1, b1, W2, b2, out):
                 h1q.pop(2 * q + 1)
 
         def add_b2(q, ip):
-            t = stream.tile([P, 2, TGT], F32, name="u", tag="u", bufs=4)
+            t = stream.tile([P, 2, TGT], F32, name="u", tag="u", bufs=3)
             nc.vector.tensor_tensor(out=t[:], in0=ps2.pop((q, ip))[:], in1=b2d[:, q % 4, :, :], op=ALU.add)
             u_t[(q, ip)] = t
 

from contextlib import ExitStack

import concourse.mybir as mybir
from concourse.masks import make_identity

N_TOK, HID, SRC, TGT = 12288, 1024, 4, 256
FLOPS = 2 * N_TOK * HID * HID * SRC + 2 * N_TOK * HID * TGT * SRC

F32 = mybir.dt.float32
BF16 = mybir.dt.bfloat16
U32 = mybir.dt.uint32
U8 = mybir.dt.uint8
FP8X4 = mybir.dt.float8_e4m3fn_x4
ACT = mybir.ActivationFunctionType
ALU = mybir.AluOpType

P = 128
BLK = 512
NBLK = N_TOK // BLK
STEPS = NBLK * SRC * 2
S_IL = 0


def tile_moe_pb_l_kernel(tc, encodings, alphas, W1, b1, W2, b2, out):
    nc = tc.nc
    with ExitStack() as ctx:
        keep = ctx.enter_context(tc.tile_pool(name="keep", bufs=1))
        stream = ctx.enter_context(tc.tile_pool(name="stream", bufs=2))
        ps1_pool = ctx.enter_context(tc.psum_pool(name="ps1p", bufs=4))
        ps2_pool = ctx.enter_context(tc.psum_pool(name="ps2p", bufs=2))
        xt_pool = ctx.enter_context(tc.psum_pool(name="xtp", bufs=2))
        ctx.enter_context(tc.manual_schedule())

        w1c = keep.tile([P, SRC, 2, HID], U32, name="w1c", align_bytes=64)
        w1s = keep.tile([P, SRC, 2, HID], U8, name="w1s", align_bytes=64)
        w2c = keep.tile([P, SRC, 2 * TGT], U32, name="w2c", align_bytes=64)
        w2s = keep.tile([P, SRC, 2 * TGT], U8, name="w2s", align_bytes=64)
        ident = keep.tile([P, P], F32, name="ident")
        ones = keep.tile([P, P], BF16, name="ones")
        bz = keep.tile([P, SRC * TGT], BF16, name="bz")
        b1raw = keep.tile([P, SRC, 16], BF16, name="b1raw")
        b1col = keep.tile([P, SRC, 8], F32, name="b1col")
        b2d = keep.tile([P, SRC, 2, TGT], F32, name="b2d")
        a_sb = keep.tile([P, BLK], BF16, name="a_sb")
        a32 = keep.tile([P, 4, P], F32, name="a32")
        acol = keep.tile([P, 4, P], F32, name="acol")
        warm = keep.tile([P, 1], F32, name="warm")

        x_raw = {}
        x_relu = {}
        x_grp = {}
        h0 = {}
        w1raw = {}
        w1grp = {}
        w2raw = {}
        w2grp = {}
        h1r = {}
        h1g = {}
        h1q = {}
        ps2 = {}
        u_t = {}
        acc = {}

        def load_x(b):
            t = stream.tile([P, 4 * HID], BF16, name="xraw", tag="xraw", bufs=2)
            nc.sync.dma_start(out=t[:], in_=encodings[b * BLK:(b + 1) * BLK, :].rearrange("(p i) h -> p (i h)", i=4))
            x_raw[b] = t

        def relu_x(b):
            t = stream.tile([P, 4 * HID], BF16, name="xsort", tag="xsort", bufs=2)
            nc.vector.tensor_scalar_max(out=t[:].rearrange("p (u m e) -> p m u e", u=2, e=2),
                                        in0=x_raw.pop(b)[:].rearrange("p (m u e) -> p m u e", u=2, e=2), scalar1=0.0)
            x_relu[b] = t

        def transpose_x(b, g, copy_engines):
            words = x_relu[b][:].bitcast(F32)
            if g == 0:
                x_grp[b] = stream.tile([P, 2 * BLK * 4], BF16, name="xgrp", tag="xgrp", bufs=2, align_bytes=64)
            gw = x_grp[b][:].bitcast(F32)
            for ip in range(2):
                xt = xt_pool.tile([P, 2, 2 * P], F32, name="xt", tag="xt")
                for i2 in range(2):
                    i = 2 * ip + i2
                    for u in range(2):
                        lo = 1024 * u + P * (2 * i + g)
                        nc.tensor.transpose(xt[:, u, P * i2:P * (i2 + 1)], words[:, lo:lo + P], ident[:])
                dst = gw[:, 1024 * g + 512 * ip:1024 * g + 512 * (ip + 1)].rearrange("p (c u) -> p c u", u=2)
                src = xt[:].rearrange("p u c -> p c u")
                if copy_engines[ip] == "s":
                    nc.scalar.copy(out=dst, in_=src)
                else:
                    nc.vector.tensor_copy(out=dst, in_=src)
            if g == 1:
                x_relu.pop(b)

        def quant_x(b, g):
            if g == 0:
                hc = stream.tile([P, 2, BLK], U32, name="h0c", tag="h0c", bufs=2, align_bytes=64)
                hs = stream.tile([P, 2, BLK], U8, name="h0s", tag="h0s", bufs=2, align_bytes=64)
                h0[b] = (hc, hs)
            hc, hs = h0[b]
            nc.vector.quantize_mx(out=hc[:, g, :].bitcast(FP8X4), scales=hs[:, g, :],
                                  in_=x_grp[b][:, 2048 * g:2048 * (g + 1)])
            if g == 1:
                x_grp.pop(b)

        def load_w1(s, g):
            t = stream.tile([P, 4 * HID], BF16, name="w1raw", tag="w1raw", bufs=4)
            nc.sync.dma_start(out=t[:], in_=W1[s, 512 * g:512 * (g + 1), :].rearrange("(p j) c -> p (j c)", j=4))
            w1raw[(s, g)] = t

        def il_w1(eng, s, g, hh):
            t = stream.tile([P, 2048], BF16, name="wgrp", tag="wgrp", bufs=3, align_bytes=64)
            dst = t[:].rearrange("p (t m j) -> p t m j", t=4, j=4)
            src = w1raw[(s, g)][:].rearrange("p (j c) -> p j c", j=4)[:, :, 512 * hh:512 * (hh + 1)].rearrange(
                "p j (m t) -> p t m j", t=4)
            if eng == "v":
                nc.vector.tensor_copy(out=dst, in_=src)
            elif eng == "s":
                nc.scalar.copy(out=dst, in_=src)
            else:
                nc.gpsimd.tensor_scalar(out=dst, in0=src, scalar1=1.0, scalar2=0.0, op0=ALU.mult, op1=ALU.add)
            w1grp[(s, g, hh)] = t

        def q_w1(s, g, hh):
            cols = (512 * hh, 512 * (hh + 1))
            nc.vector.quantize_mx(out=w1c[:, s, g, cols[0]:cols[1]].bitcast(FP8X4),
                                  scales=w1s[:, s, g, cols[0]:cols[1]], in_=w1grp.pop((s, g, hh))[:])

        def load_w2(s):
            t = stream.tile([P, 2, 4 * TGT], BF16, name="w2raw", tag="w2raw", bufs=2)
            nc.sync.dma_start(out=t[:], in_=W2[s, :, :].rearrange("(g p j) t -> p g (j t)", g=2, j=4))
            w2raw[s] = t

        def il_w2(eng, s):
            t = stream.tile([P, 2048], BF16, name="w2grp", tag="w2grp", bufs=2, align_bytes=64)
            dst = t[:].rearrange("p (g t j) -> p g t j", g=2, j=4)
            src = w2raw.pop(s)[:].rearrange("p g (j t) -> p g t j", j=4)
            if eng == "v":
                nc.vector.tensor_copy(out=dst, in_=src)
            else:
                nc.gpsimd.tensor_scalar(out=dst, in0=src, scalar1=1.0, scalar2=0.0, op0=ALU.mult, op1=ALU.add)
            w2grp[s] = t

        def q_w2(s):
            nc.vector.quantize_mx(out=w2c[:, s, :].bitcast(FP8X4), scales=w2s[:, s, :], in_=w2grp.pop(s)[:])

        def stage1(hstep):
            b, s, hh = hstep // 8, (hstep // 2) % 4, hstep % 2
            hc, hs = h0[b]
            r = stream.tile([P, 4, BLK], BF16, name="h1r", tag="h1r", bufs=3)
            for t in range(4):
                ps = ps1_pool.tile([P, BLK], F32, name="ps1", tag="ps1")
                lo = 512 * hh + P * t
                for g in range(2):
                    nc.tensor.matmul_mx(out=ps[:], lhsT=w1c[:, s, g, lo:lo + P].bitcast(FP8X4),
                                        lhsT_scale=w1s[:, s, g, lo:lo + P],
                                        rhs=hc[:, g, :].bitcast(FP8X4), rhs_scale=hs[:, g, :],
                                        start=(g == 0), stop=(g == 1))
                nc.scalar.activation(out=r[:, t, :], in_=ps[:], func=ACT.Relu,
                                     bias=b1col[:, s, 4 * hh + t:4 * hh + t + 1])
            h1r[hstep] = r
            if hstep % 8 == 7:
                h0.pop(b)

        def il_h1(hstep):
            t = stream.tile([P, BLK, 4], BF16, name="h1g", tag="h1g", bufs=2, align_bytes=64)
            src = h1r.pop(hstep)[:].rearrange("p t (c i) -> p c t i", i=4)
            dst = t[:].rearrange("p (c i) t -> p c t i", i=4)
            cut = (BLK - S_IL) // 4
            nc.vector.tensor_copy(out=dst[:, 0:cut, :, :], in_=src[:, 0:cut, :, :])
            if S_IL > 0:
                nc.scalar.copy(out=dst[:, cut:BLK // 4, :, :], in_=src[:, cut:BLK // 4, :, :])
            h1g[hstep] = t

        def q_h1(hstep):
            c = stream.tile([P, BLK], U32, name="h1c", tag="h1c", bufs=5, align_bytes=64)
            sc = stream.tile([P, BLK], U8, name="h1s", tag="h1s", bufs=5, align_bytes=64)
            nc.vector.quantize_mx(out=c[:].bitcast(FP8X4), scales=sc[:],
                                  in_=h1g.pop(hstep)[:].rearrange("p c t -> p (c t)"))
            h1q[hstep] = (c, sc)

        def stage2(q, ip):
            s = q % 4
            ps = ps2_pool.tile([P, 2, TGT], F32, name="ps2", tag="ps2")
            for i2 in range(2):
                lo = P * (2 * ip + i2)
                for hh in range(2):
                    c, sc = h1q[2 * q + hh]
                    nc.tensor.matmul_mx(out=ps[:, i2, :], lhsT=c[:, lo:lo + P].bitcast(FP8X4),
                                        lhsT_scale=sc[:, lo:lo + P],
                                        rhs=w2c[:, s, TGT * hh:TGT * (hh + 1)].bitcast(FP8X4),
                                        rhs_scale=w2s[:, s, TGT * hh:TGT * (hh + 1)],
                                        start=(hh == 0), stop=(hh == 1))
            ps2[(q, ip)] = ps
            if ip == 1:
                h1q.pop(2 * q)
                h1q.pop(2 * q + 1)

        def add_b2(q, ip):
            t = stream.tile([P, 2, TGT], F32, name="u", tag="u", bufs=3)
            nc.vector.tensor_tensor(out=t[:], in0=ps2.pop((q, ip))[:], in1=b2d[:, q % 4, :, :], op=ALU.add)
            u_t[(q, ip)] = t

        def sigmoid(q, ip):
            t = u_t[(q, ip)]
            nc.scalar.activation(out=t[:], in_=t[:], func=ACT.Sigmoid)

        def wsum(q, ip):
            b, s = q // 4, q % 4
            if s == 0 and ip == 0:
                acc[b] = stream.tile([P, 4, TGT], F32, name="acc", tag="acc", bufs=2)
            a = acc[b]
            t = u_t.pop((q, ip))
            for i2 in range(2):
                i = 2 * ip + i2
                col = acol[:, i, NBLK * s + b:NBLK * s + b + 1]
                if s == 0:
                    nc.vector.tensor_scalar_mul(out=a[:, i, :], in0=t[:, i2, :], scalar1=col)
                else:
                    nc.vector.scalar_tensor_tensor(out=a[:, i, :], in0=t[:, i2, :], scalar=col, in1=a[:, i, :],
                                                   op0=ALU.mult, op1=ALU.add)
            if s == 3 and ip == 1:
                nc.sync.dma_start(out=out[b * BLK:(b + 1) * BLK, :].rearrange("(p i) t -> p (i t)", i=4),
                                  in_=acc.pop(b)[:].rearrange("p i t -> p (i t)"))

        nc.vector.memset(warm[:], 0.0)
        nc.vector.memset(bz[:], 0.0)
        nc.vector.memset(a_sb[:], 0.0)
        nc.vector.memset(ones[:], 1.0)
        nc.scalar.dma_start(out=a_sb[0:96, :], in_=alphas.rearrange("s (b c) -> (s b) c", c=BLK))
        nc.scalar.dma_start(out=bz[0:1, :], in_=b2.rearrange("(o s) t -> o (s t)", o=1))
        for s in range(SRC):
            nc.scalar.dma_start(out=b1raw[:, s, 0:8].rearrange("p (g t) -> p g t", g=2),
                                in_=b1[s, :].rearrange("(g p t) -> p g t", g=2, t=4))
        nc.scalar.activation(out=warm[:], in_=warm[:], func=ACT.Sigmoid)
        load_x(0)
        load_w1(0, 0)
        load_w1(0, 1)
        load_w1(1, 0)
        load_w1(1, 1)
        load_x(1)
        load_w2(0)
        make_identity(nc, ident[:])

        nc.vector.tensor_copy(out=a32[:], in_=a_sb[:].rearrange("r (p i) -> r i p", i=4))
        pa = xt_pool.tile([P, 4, P], F32, name="xt", tag="xt")
        for i in range(4):
            nc.tensor.transpose(pa[:, i, :], a32[:, i, :], ident[:])
        nc.vector.tensor_copy(out=acol[:], in_=pa[:])
        for h in range(2):
            pb = xt_pool.tile([P, 2, TGT], F32, name="xt", tag="xt")
            nc.tensor.matmul(out=pb[:].rearrange("p s t -> p (s t)"), lhsT=ones[:], rhs=bz[:, 512 * h:512 * (h + 1)],
                             start=True, stop=True)
            for d in range(2):
                nc.vector.tensor_copy(out=b2d[:, 2 * h:2 * h + 2, d, :], in_=pb[:])
        nc.vector.tensor_copy(out=b1col[:], in_=b1raw[:, :, 0:8])

        relu_x(0)
        transpose_x(0, 0, ("s", "s"))
        il_w1("v", 0, 0, 0)
        transpose_x(0, 1, ("s", "s"))
        quant_x(0, 0)
        q_w1(0, 0, 0)
        il_w1("v", 0, 1, 0)
        il_w1("s", 0, 0, 1)
        quant_x(0, 1)
        q_w1(0, 1, 0)
        il_w1("s", 0, 1, 1)
        q_w1(0, 0, 1)

        for hs_i in range(STEPS + 6):
            b, r8 = hs_i // 8, hs_i % 8
            if hs_i == 0:
                load_w2(1)
                load_w1(2, 0)
                load_w1(2, 1)
            if hs_i == 2:
                load_w2(2)
                load_w1(3, 0)
                load_w1(3, 1)
            if hs_i == 4:
                load_w2(3)
            k = hs_i - 2
            if k >= 3 and k < STEPS + 3:
                sigmoid((k - 3) // 2, (k - 3) % 2)
            k = hs_i - 1
            if k >= 3 and k < STEPS + 3:
                add_b2((k - 3) // 2, (k - 3) % 2)
            if hs_i < STEPS:
                stage1(hs_i)
            if hs_i >= 1 and hs_i - 1 < STEPS:
                il_h1(hs_i - 1)
            k = hs_i - 3
            if k >= 3 and k < STEPS + 3:
                wsum((k - 3) // 2, (k - 3) % 2)
            if hs_i >= 1 and hs_i - 1 < STEPS:
                q_h1(hs_i - 1)
            if hs_i >= 3 and hs_i < STEPS + 3:
                stage2((hs_i - 3) // 2, (hs_i - 3) % 2)
            if b + 1 < NBLK:
                if r8 == 1:
                    relu_x(b + 1)
                if r8 == 2:
                    transpose_x(b + 1, 0, ("s", "s"))
                if r8 == 3:
                    quant_x(b + 1, 0)
                if r8 == 4:
                    transpose_x(b + 1, 1, ("s", "s"))
                if r8 == 5:
                    quant_x(b + 1, 1)
                    if b + 2 < NBLK:
                        load_x(b + 2)
            if hs_i == 0:
                q_w1(0, 1, 1)
                il_w2("v", 0)
            if hs_i < 6:
                s, hh = hs_i // 2 + 1, hs_i % 2
                if hs_i >= 1:
                    q_w1((hs_i - 1) // 2 + 1, 1, (hs_i - 1) % 2)
                il_w1("v", s, 0, hh)
                il_w1("s", s, 1, hh)
                q_w1(s, 0, hh)
            if hs_i == 6:
                q_w1(3, 1, 1)
            if hs_i < 8 and hs_i % 2 == 0 and hs_i >= 2:
                il_w2("v", hs_i // 2)
            if hs_i < 8 and hs_i % 2 == 1:
                q_w2(hs_i // 2)
